import numpy as np
import ml_dtypes


def mxq(x, axis, fmt="e4m3"):
    dtype, down = {"e4m3": (ml_dtypes.float8_e4m3fn, 7), "e5m2": (ml_dtypes.float8_e5m2, 14)}[fmt]
    v = np.moveaxis(np.asarray(x, np.float32).astype(ml_dtypes.bfloat16).astype(np.float64), axis, -1)
    blocks = v.reshape(v.shape[:-1] + (-1, 32))
    amax = np.abs(blocks).max(-1, keepdims=True)
    byte = np.maximum(np.where(amax > 0, np.frexp(amax)[1] - 1 + 127, 0) - down, 1)
    scale = np.exp2(byte - 127.0)
    codes = (blocks / scale).astype(np.float32).astype(dtype).astype(np.float64)
    return np.moveaxis((codes * scale).reshape(v.shape), -1, axis)


WIDE = False


def mx_kscale(k):
    if not WIDE:
        return np.ones(k)
    levels = np.array([10, -10, 5, -5, 0])
    a = np.random.permutation(np.resize(levels, k // 512 * 4)).reshape(k // 512, 4)
    idx = np.arange(k)
    return np.exp2(a[idx // 512, idx % 128 // 32])


BF16 = ml_dtypes.bfloat16


def bf(x):
    return np.asarray(x, np.float32).astype(BF16)


def f64(x):
    return np.asarray(x).astype(np.float64)


B, S, D, P, PW, L = 2, 192, 512, 4, 2, 2


def sigmoid(v):
    return 1.0 / (1.0 + np.exp(-v))


def setup_inputs():
    n = np.random.standard_normal
    s = mx_kscale(D)
    return {"x": bf(n((B, S, D)) * s),
            "amp_w": bf(n((D, D)) / np.sqrt(D) / s[:, None]),
            "amp_b": bf(n(D) * 0.3),
            "ph_w": bf(n((D, D)) / np.sqrt(D) / s[:, None]),
            "ph_b": bf(n(D) * 0.3)}


def reference(x, amp_w, amp_b, ph_w, ph_b):
    xq = mxq(f64(x), 2, "e4m3")
    amp = sigmoid((xq @ mxq(f64(amp_w), 0, "e4m3")) + f64(amp_b))
    ph = np.tanh((xq @ mxq(f64(ph_w), 0, "e4m3")) + f64(ph_b)) * np.pi
    return (np.cos(ph) + np.sin(ph)) * amp

@@ -1,0 +1,201 @@
+import math
+from contextlib import ExitStack
+
+import concourse.mybir as mybir
+from concourse.masks import make_identity
+
+F32 = mybir.dt.float32
+BF16 = mybir.dt.bfloat16
+U32 = mybir.dt.uint32
+U8 = mybir.dt.uint8
+FP8X4 = mybir.dt.float8_e4m3fn_x4
+ACT = mybir.ActivationFunctionType
+ALU = mybir.AluOpType
+
+P = 128
+PACK = 4
+K = P * PACK
+TOKENS = 384
+TOKEN_TILES = TOKENS // P
+FEATURES = 512
+FEATURE_TILES = FEATURES // P
+WIDE = 256
+
+FLOPS = 2 * TOKENS * K * 2 * FEATURES
+
+
+def load_weight(nc, pool, weight, name):
+    raw = pool.tile([P, PACK, FEATURES], BF16, name=name)
+    nc.sync.dma_start(out=raw[:], in_=weight.rearrange("(p t) n -> p t n", t=PACK))
+    return raw
+
+
+def quantise_weight(nc, pool, raw, name):
+    grouped = pool.tile([P, FEATURES, PACK], BF16, name=name + "_grouped", align_bytes=64)
+    codes = pool.tile([P, FEATURES], U32, name=name + "_codes", align_bytes=64)
+    scales = pool.tile([P, FEATURES], U8, name=name + "_scales", align_bytes=64)
+    for f in range(FEATURE_TILES):
+        cols = slice(f * P, (f + 1) * P)
+        nc.vector.tensor_copy(
+            out=grouped[:, cols, :].rearrange("p (c i) t -> p c t i", i=4),
+            in_=raw[:, :, cols].rearrange("p t (c i) -> p c t i", i=4),
+        )
+    for f in range(FEATURE_TILES):
+        cols = slice(f * P, (f + 1) * P)
+        nc.vector.quantize_mx(
+            out=codes[:, cols].bitcast(FP8X4),
+            scales=scales[:, cols],
+            in_=grouped[:, cols, :].rearrange("p c t -> p (c t)"),
+        )
+    return codes, scales
+
+
+def multiply(nc, banks, w_codes, w_scales, x_codes, x_scales, f, name):
+    features = slice(f * P, (f + 1) * P)
+    product = banks.tile([P, TOKENS], F32, tag="bank", name=name)
+    for tokens in (slice(0, WIDE), slice(WIDE, TOKENS)):
+        nc.tensor.matmul_mx(
+            out=product[:, tokens],
+            lhsT=w_codes[:, features].bitcast(FP8X4),
+            lhsT_scale=w_scales[:, features],
+            rhs=x_codes[:, tokens].bitcast(FP8X4),
+            rhs_scale=x_scales[:, tokens],
+            start=True,
+            stop=True,
+        )
+    return product
+
+
+def tile_quantuminspiredneuralcore_pa_s_kernel(tc, x, amp_w, amp_b, ph_w, ph_b, out):
+    nc = tc.nc
+    x_rows = x.flatten_outer_dims().rearrange("(p a) k -> p a k", a=TOKEN_TILES)
+    out_rows = out.flatten_outer_dims().rearrange("(p a) n -> p a n", a=TOKEN_TILES)
+
+    with ExitStack() as stack:
+        keep = stack.enter_context(tc.tile_pool(name="keep", bufs=1))
+        banks = stack.enter_context(tc.psum_pool(name="banks", bufs=8))
+
+        x_sb = keep.tile([P, TOKEN_TILES, K], BF16)
+        nc.sync.dma_start(out=x_sb[:], in_=x_rows)
+        ph_raw = load_weight(nc, keep, ph_w, "ph_raw")
+        amp_raw = load_weight(nc, keep, amp_w, "amp_raw")
+        bias_rows = keep.tile([P, P], BF16)
+        nc.vector.memset(bias_rows[:], 0.0)
+        nc.scalar.dma_start(
+            out=bias_rows[0:FEATURE_TILES, :], in_=amp_b.rearrange("(f c) -> f c", c=P)
+        )
+        nc.scalar.dma_start(
+            out=bias_rows[FEATURE_TILES : 2 * FEATURE_TILES, :],
+            in_=ph_b.rearrange("(f c) -> f c", c=P),
+        )
+
+        ident_f32 = keep.tile([P, P], F32)
+        make_identity(nc, ident_f32[:])
+        ident_bf16 = keep.tile([P, P], BF16)
+        make_identity(nc, ident_bf16[:])
+        one = keep.tile([P, 1], F32)
+        nc.vector.memset(one[:], 1.0)
+        unused = keep.tile([P, 1], F32)
+        nc.scalar.activation(out=unused[:], in_=one[:], func=ACT.Silu)
+
+        x_words = x_sb[:].bitcast(F32).rearrange("p a (q u) -> p a u q", u=2)
+        x_grouped = keep.tile([P, TOKENS, PACK], BF16, align_bytes=64)
+        x_grouped_words = x_grouped[:].bitcast(F32)
+        for a in range(TOKEN_TILES):
+            x_t = banks.tile([P, 2, P], F32, tag="bank", name="x_t")
+            for u in range(2):
+                nc.tensor.transpose(x_t[:, u, :], x_words[:, a, u, :], ident_f32[:])
+            nc.scalar.copy(
+                out=x_grouped_words[:, a * P : (a + 1) * P, :],
+                in_=x_t[:].rearrange("q u c -> q c u"),
+            )
+        x_codes = keep.tile([P, TOKENS], U32, align_bytes=64)
+        x_scales = keep.tile([P, TOKENS], U8, align_bytes=64)
+        for tokens in (slice(0, WIDE), slice(WIDE, TOKENS)):
+            nc.vector.quantize_mx(
+                out=x_codes[:, tokens].bitcast(FP8X4),
+                scales=x_scales[:, tokens],
+                in_=x_grouped[:, tokens, :].rearrange("p c t -> p (c t)"),
+            )
+
+        bias_t = banks.tile([P, P], BF16, tag="bank", name="bias_t")
+        nc.tensor.transpose(bias_t[:], bias_rows[:], ident_bf16[:])
+        half_amp_bias = keep.tile([P, FEATURE_TILES], F32)
+        nc.vector.tensor_scalar(
+            out=half_amp_bias[:],
+            in0=bias_t[:, 0:FEATURE_TILES],
+            scalar1=0.5,
+            scalar2=None,
+            op0=ALU.mult,
+        )
+        ph_bias = keep.tile([P, FEATURE_TILES], F32)
+        nc.vector.tensor_copy(out=ph_bias[:], in_=bias_t[:, FEATURE_TILES : 2 * FEATURE_TILES])
+
+        tanh_ph = keep.tile([P, FEATURE_TILES, TOKENS], F32)
+        tanh_amp = keep.tile([P, FEATURE_TILES, TOKENS], F32)
+        ph_codes, ph_scales = quantise_weight(nc, keep, ph_raw, "ph")
+        for f in range(FEATURE_TILES):
+            product = multiply(nc, banks, ph_codes, ph_scales, x_codes, x_scales, f, "ph_product")
+            nc.scalar.activation(
+                out=tanh_ph[:, f, :], in_=product[:], func=ACT.Tanh, bias=ph_bias[:, f : f + 1]
+            )
+        amp_codes, amp_scales = quantise_weight(nc, keep, amp_raw, "amp")
+        for f in range(FEATURE_TILES):
+            product = multiply(nc, banks, amp_codes, amp_scales, x_codes, x_scales, f, "amp_product")
+            nc.scalar.activation(
+                out=tanh_amp[:, f, :],
+                in_=product[:],
+                func=ACT.Tanh,
+                bias=half_amp_bias[:, f : f + 1],
+                scale=0.5,
+            )
+
+        mirrored = keep.tile([P, FEATURE_TILES, TOKENS], F32)
+        folded = keep.tile([P, FEATURE_TILES, TOKENS], F32)
+        sine = keep.tile([P, FEATURE_TILES, TOKENS], F32)
+        value = keep.tile([P, FEATURE_TILES, TOKENS], F32)
+        result = keep.tile([P, TOKEN_TILES, FEATURES], F32)
+        for f in range(FEATURE_TILES):
+            nc.vector.tensor_scalar(
+                out=mirrored[:, f, :],
+                in0=tanh_ph[:, f, :],
+                scalar1=-1.0,
+                scalar2=0.75,
+                op0=ALU.mult,
+                op1=ALU.add,
+            )
+            nc.vector.scalar_tensor_tensor(
+                out=folded[:, f, :],
+                in0=tanh_ph[:, f, :],
+                scalar=0.25,
+                in1=mirrored[:, f, :],
+                op0=ALU.add,
+                op1=ALU.min,
+            )
+        for f in range(FEATURE_TILES):
+            features = slice(f * P, (f + 1) * P)
+            nc.scalar.activation(
+                out=sine[:, f, :], in_=folded[:, f, :], func=ACT.Sin, scale=math.pi
+            )
+            nc.vector.scalar_tensor_tensor(
+                out=value[:, f, :],
+                in0=tanh_amp[:, f, :],
+                scalar=1.0,
+                in1=sine[:, f, :],
+                op0=ALU.add,
+                op1=ALU.mult,
+            )
+            value_t = banks.tile([P, TOKEN_TILES, P], F32, tag="bank", name="value_t")
+            for a in range(TOKEN_TILES):
+                nc.tensor.transpose(value_t[:, a, :], value[:, f, a * P : (a + 1) * P], ident_f32[:])
+            if f % 2 == 0:
+                nc.scalar.mul(out=result[:, :, features], in_=value_t[:], mul=1.0 / math.sqrt(2.0))
+            else:
+                nc.vector.tensor_scalar(
+                    out=result[:, :, features],
+                    in0=value_t[:],
+                    scalar1=1.0 / math.sqrt(2.0),
+                    scalar2=None,
+                    op0=ALU.mult,
+                )
+            nc.sync.dma_start(out=out_rows[:, :, features], in_=result[:, :, features])

@@ -19,9 +19,13 @@ TOKENS = 384
 TOKEN_TILES = TOKENS // P
 FEATURES = 512
 FEATURE_TILES = FEATURES // P
-WIDE = 256
+HALF = 256
 
 FLOPS = 2 * TOKENS * K * 2 * FEATURES
+
+
+def tile_of(f):
+    return slice(f * P, (f + 1) * P)
 
 
 def load_weight(nc, pool, weight, name):
@@ -30,34 +34,28 @@ def load_weight(nc, pool, weight, name):
     return raw
 
 
-def quantise_weight(nc, pool, raw, name):
-    grouped = pool.tile([P, FEATURES, PACK], BF16, name=name + "_grouped", align_bytes=64)
-    codes = pool.tile([P, FEATURES], U32, name=name + "_codes", align_bytes=64)
-    scales = pool.tile([P, FEATURES], U8, name=name + "_scales", align_bytes=64)
-    for f in range(FEATURE_TILES):
-        cols = slice(f * P, (f + 1) * P)
-        nc.vector.tensor_copy(
-            out=grouped[:, cols, :].rearrange("p (c i) t -> p c t i", i=4),
-            in_=raw[:, :, cols].rearrange("p t (c i) -> p c t i", i=4),
-        )
-    for f in range(FEATURE_TILES):
-        cols = slice(f * P, (f + 1) * P)
-        nc.vector.quantize_mx(
-            out=codes[:, cols].bitcast(FP8X4),
-            scales=scales[:, cols],
-            in_=grouped[:, cols, :].rearrange("p c t -> p (c t)"),
-        )
-    return codes, scales
+def regroup(copy, grouped, raw, cols):
+    copy(
+        out=grouped[:, cols, :].rearrange("p (c i) t -> p c t i", i=4),
+        in_=raw[:, :, cols].rearrange("p t (c i) -> p c t i", i=4),
+    )
+
+
+def quantise(nc, codes, scales, grouped, cols):
+    nc.vector.quantize_mx(
+        out=codes[:, cols].bitcast(FP8X4),
+        scales=scales[:, cols],
+        in_=grouped[:, cols, :].rearrange("p c t -> p (c t)"),
+    )
 
 
 def multiply(nc, banks, w_codes, w_scales, x_codes, x_scales, f, name):
-    features = slice(f * P, (f + 1) * P)
     product = banks.tile([P, TOKENS], F32, tag="bank", name=name)
-    for tokens in (slice(0, WIDE), slice(WIDE, TOKENS)):
+    for tokens in (slice(0, HALF), slice(HALF, TOKENS)):
         nc.tensor.matmul_mx(
             out=product[:, tokens],
-            lhsT=w_codes[:, features].bitcast(FP8X4),
-            lhsT_scale=w_scales[:, features],
+            lhsT=w_codes[:, tile_of(f)].bitcast(FP8X4),
+            lhsT_scale=w_scales[:, tile_of(f)],
             rhs=x_codes[:, tokens].bitcast(FP8X4),
             rhs_scale=x_scales[:, tokens],
             start=True,
@@ -70,14 +68,18 @@ def tile_quantuminspiredneuralcore_pa_s_kernel(tc, x, amp_w, amp_b, ph_w, ph_b, 
     nc = tc.nc
     x_rows = x.flatten_outer_dims().rearrange("(p a) k -> p a k", a=TOKEN_TILES)
     out_rows = out.flatten_outer_dims().rearrange("(p a) n -> p a n", a=TOKEN_TILES)
+    first_half = slice(0, HALF)
+    second_half = slice(HALF, FEATURES)
 
     with ExitStack() as stack:
         keep = stack.enter_context(tc.tile_pool(name="keep", bufs=1))
         banks = stack.enter_context(tc.psum_pool(name="banks", bufs=8))
+        stack.enter_context(tc.manual_schedule())
 
-        x_sb = keep.tile([P, TOKEN_TILES, K], BF16)
-        nc.sync.dma_start(out=x_sb[:], in_=x_rows)
         ph_raw = load_weight(nc, keep, ph_w, "ph_raw")
+        x_sb = keep.tile([P, TOKEN_TILES, K], BF16)
+        for a in range(TOKEN_TILES):
+            nc.sync.dma_start(out=x_sb[:, a, :], in_=x_rows[:, a, :])
         amp_raw = load_weight(nc, keep, amp_w, "amp_raw")
         bias_rows = keep.tile([P, P], BF16)
         nc.vector.memset(bias_rows[:], 0.0)
@@ -98,6 +100,15 @@ def tile_quantuminspiredneuralcore_pa_s_kernel(tc, x, amp_w, amp_b, ph_w, ph_b, 
         unused = keep.tile([P, 1], F32)
         nc.scalar.activation(out=unused[:], in_=one[:], func=ACT.Silu)
 
+        ph_grouped = keep.tile([P, FEATURES, PACK], BF16, align_bytes=64)
+        ph_codes = keep.tile([P, FEATURES], U32, align_bytes=64)
+        ph_scales = keep.tile([P, FEATURES], U8, align_bytes=64)
+        regroup(nc.vector.tensor_copy, ph_grouped, ph_raw, first_half)
+        regroup(nc.vector.tensor_copy, ph_grouped, ph_raw, tile_of(2))
+        regroup(nc.scalar.copy, ph_grouped, ph_raw, tile_of(3))
+        quantise(nc, ph_codes, ph_scales, ph_grouped, first_half)
+        quantise(nc, ph_codes, ph_scales, ph_grouped, second_half)
+
         x_words = x_sb[:].bitcast(F32).rearrange("p a (q u) -> p a u q", u=2)
         x_grouped = keep.tile([P, TOKENS, PACK], BF16, align_bytes=64)
         x_grouped_words = x_grouped[:].bitcast(F32)
@@ -106,40 +117,36 @@ def tile_quantuminspiredneuralcore_pa_s_kernel(tc, x, amp_w, amp_b, ph_w, ph_b, 
             for u in range(2):
                 nc.tensor.transpose(x_t[:, u, :], x_words[:, a, u, :], ident_f32[:])
             nc.scalar.copy(
-                out=x_grouped_words[:, a * P : (a + 1) * P, :],
-                in_=x_t[:].rearrange("q u c -> q c u"),
-            )
-        x_codes = keep.tile([P, TOKENS], U32, align_bytes=64)
-        x_scales = keep.tile([P, TOKENS], U8, align_bytes=64)
-        for tokens in (slice(0, WIDE), slice(WIDE, TOKENS)):
-            nc.vector.quantize_mx(
-                out=x_codes[:, tokens].bitcast(FP8X4),
-                scales=x_scales[:, tokens],
-                in_=x_grouped[:, tokens, :].rearrange("p c t -> p (c t)"),
+                out=x_grouped_words[:, tile_of(a), :], in_=x_t[:].rearrange("q u c -> q c u")
             )
 
         bias_t = banks.tile([P, P], BF16, tag="bank", name="bias_t")
         nc.tensor.transpose(bias_t[:], bias_rows[:], ident_bf16[:])
         half_amp_bias = keep.tile([P, FEATURE_TILES], F32)
-        nc.vector.tensor_scalar(
-            out=half_amp_bias[:],
-            in0=bias_t[:, 0:FEATURE_TILES],
-            scalar1=0.5,
-            scalar2=None,
-            op0=ALU.mult,
-        )
+        nc.scalar.mul(out=half_amp_bias[:], in_=bias_t[:, 0:FEATURE_TILES], mul=0.5)
         ph_bias = keep.tile([P, FEATURE_TILES], F32)
-        nc.vector.tensor_copy(out=ph_bias[:], in_=bias_t[:, FEATURE_TILES : 2 * FEATURE_TILES])
+        nc.scalar.copy(out=ph_bias[:], in_=bias_t[:, FEATURE_TILES : 2 * FEATURE_TILES])
+
+        x_codes = keep.tile([P, TOKENS], U32, align_bytes=64)
+        x_scales = keep.tile([P, TOKENS], U8, align_bytes=64)
+        quantise(nc, x_codes, x_scales, x_grouped, slice(0, HALF))
+        quantise(nc, x_codes, x_scales, x_grouped, slice(HALF, TOKENS))
 
         tanh_ph = keep.tile([P, FEATURE_TILES, TOKENS], F32)
-        tanh_amp = keep.tile([P, FEATURE_TILES, TOKENS], F32)
-        ph_codes, ph_scales = quantise_weight(nc, keep, ph_raw, "ph")
         for f in range(FEATURE_TILES):
             product = multiply(nc, banks, ph_codes, ph_scales, x_codes, x_scales, f, "ph_product")
             nc.scalar.activation(
                 out=tanh_ph[:, f, :], in_=product[:], func=ACT.Tanh, bias=ph_bias[:, f : f + 1]
             )
-        amp_codes, amp_scales = quantise_weight(nc, keep, amp_raw, "amp")
+
+        amp_grouped = keep.tile([P, FEATURES, PACK], BF16, align_bytes=64)
+        amp_codes = keep.tile([P, FEATURES], U32, align_bytes=64)
+        amp_scales = keep.tile([P, FEATURES], U8, align_bytes=64)
+        regroup(nc.vector.tensor_copy, amp_grouped, amp_raw, first_half)
+        regroup(nc.vector.tensor_copy, amp_grouped, amp_raw, second_half)
+        quantise(nc, amp_codes, amp_scales, amp_grouped, first_half)
+        quantise(nc, amp_codes, amp_scales, amp_grouped, second_half)
+        tanh_amp = keep.tile([P, FEATURE_TILES, TOKENS], F32)
         for f in range(FEATURE_TILES):
             product = multiply(nc, banks, amp_codes, amp_scales, x_codes, x_scales, f, "amp_product")
             nc.scalar.activation(
@@ -152,9 +159,6 @@ def tile_quantuminspiredneuralcore_pa_s_kernel(tc, x, amp_w, amp_b, ph_w, ph_b, 
 
         mirrored = keep.tile([P, FEATURE_TILES, TOKENS], F32)
         folded = keep.tile([P, FEATURE_TILES, TOKENS], F32)
-        sine = keep.tile([P, FEATURE_TILES, TOKENS], F32)
-        value = keep.tile([P, FEATURE_TILES, TOKENS], F32)
-        result = keep.tile([P, TOKEN_TILES, FEATURES], F32)
         for f in range(FEATURE_TILES):
             nc.vector.tensor_scalar(
                 out=mirrored[:, f, :],
@@ -172,8 +176,11 @@ def tile_quantuminspiredneuralcore_pa_s_kernel(tc, x, amp_w, amp_b, ph_w, ph_b, 
                 op0=ALU.add,
                 op1=ALU.min,
             )
+
+        sine = keep.tile([P, FEATURE_TILES, TOKENS], F32)
+        value = keep.tile([P, FEATURE_TILES, TOKENS], F32)
+        value_t = []
         for f in range(FEATURE_TILES):
-            features = slice(f * P, (f + 1) * P)
             nc.scalar.activation(
                 out=sine[:, f, :], in_=folded[:, f, :], func=ACT.Sin, scale=math.pi
             )
@@ -185,17 +192,22 @@ def tile_quantuminspiredneuralcore_pa_s_kernel(tc, x, amp_w, amp_b, ph_w, ph_b, 
                 op0=ALU.add,
                 op1=ALU.mult,
             )
-            value_t = banks.tile([P, TOKEN_TILES, P], F32, tag="bank", name="value_t")
+            value_t.append(banks.tile([P, TOKEN_TILES, P], F32, tag="bank", name="value_t"))
             for a in range(TOKEN_TILES):
-                nc.tensor.transpose(value_t[:, a, :], value[:, f, a * P : (a + 1) * P], ident_f32[:])
-            if f % 2 == 0:
-                nc.scalar.mul(out=result[:, :, features], in_=value_t[:], mul=1.0 / math.sqrt(2.0))
+                nc.tensor.transpose(value_t[f][:, a, :], value[:, f, tile_of(a)], ident_f32[:])
+
+        result = keep.tile([P, TOKEN_TILES, FEATURES], F32)
+        for f in range(FEATURE_TILES):
+            if f < FEATURE_TILES // 2:
+                nc.scalar.mul(
+                    out=result[:, :, tile_of(f)], in_=value_t[f][:], mul=1.0 / math.sqrt(2.0)
+                )
             else:
                 nc.vector.tensor_scalar(
-                    out=result[:, :, features],
-                    in0=value_t[:],
+                    out=result[:, :, tile_of(f)],
+                    in0=value_t[f][:],
                     scalar1=1.0 / math.sqrt(2.0),
                     scalar2=None,
                     op0=ALU.mult,
                 )
-            nc.sync.dma_start(out=out_rows[:, :, features], in_=result[:, :, features])
+            nc.sync.dma_start(out=out_rows[:, :, tile_of(f)], in_=result[:, :, tile_of(f)])

@@ -34,19 +34,27 @@ def load_weight(nc, pool, weight, name):
     return raw
 
 
-def regroup(copy, grouped, raw, cols):
-    copy(
-        out=grouped[:, cols, :].rearrange("p (c i) t -> p c t i", i=4),
-        in_=raw[:, :, cols].rearrange("p t (c i) -> p c t i", i=4),
-    )
-
-
 def quantise(nc, codes, scales, grouped, cols):
     nc.vector.quantize_mx(
         out=codes[:, cols].bitcast(FP8X4),
         scales=scales[:, cols],
         in_=grouped[:, cols, :].rearrange("p c t -> p (c t)"),
     )
+
+
+def quantise_weight(nc, pool, raw, name):
+    grouped = pool.tile([P, FEATURES, PACK], BF16, name=name + "_grouped", align_bytes=64)
+    codes = pool.tile([P, FEATURES], U32, name=name + "_codes", align_bytes=64)
+    scales = pool.tile([P, FEATURES], U8, name=name + "_scales", align_bytes=64)
+    halves = (slice(0, HALF), slice(HALF, FEATURES))
+    for cols in halves:
+        nc.vector.tensor_copy(
+            out=grouped[:, cols, :].rearrange("p (c i) t -> p c t i", i=4),
+            in_=raw[:, :, cols].rearrange("p t (c i) -> p c t i", i=4),
+        )
+    for cols in halves:
+        quantise(nc, codes, scales, grouped, cols)
+    return codes, scales
 
 
 def multiply(nc, banks, w_codes, w_scales, x_codes, x_scales, f, name):
@@ -64,12 +72,17 @@ def multiply(nc, banks, w_codes, w_scales, x_codes, x_scales, f, name):
     return product
 
 
+def to_token_rows(nc, banks, values, ident, name):
+    transposed = banks.tile([P, TOKEN_TILES, P], F32, tag="bank", name=name)
+    for a in range(TOKEN_TILES):
+        nc.tensor.transpose(transposed[:, a, :], values[:, tile_of(a)], ident[:])
+    return transposed
+
+
 def tile_quantuminspiredneuralcore_pa_s_kernel(tc, x, amp_w, amp_b, ph_w, ph_b, out):
     nc = tc.nc
     x_rows = x.flatten_outer_dims().rearrange("(p a) k -> p a k", a=TOKEN_TILES)
     out_rows = out.flatten_outer_dims().rearrange("(p a) n -> p a n", a=TOKEN_TILES)
-    first_half = slice(0, HALF)
-    second_half = slice(HALF, FEATURES)
 
     with ExitStack() as stack:
         keep = stack.enter_context(tc.tile_pool(name="keep", bufs=1))
@@ -100,14 +113,7 @@ def tile_quantuminspiredneuralcore_pa_s_kernel(tc, x, amp_w, amp_b, ph_w, ph_b, 
         unused = keep.tile([P, 1], F32)
         nc.scalar.activation(out=unused[:], in_=one[:], func=ACT.Silu)
 
-        ph_grouped = keep.tile([P, FEATURES, PACK], BF16, align_bytes=64)
-        ph_codes = keep.tile([P, FEATURES], U32, align_bytes=64)
-        ph_scales = keep.tile([P, FEATURES], U8, align_bytes=64)
-        regroup(nc.vector.tensor_copy, ph_grouped, ph_raw, first_half)
-        regroup(nc.vector.tensor_copy, ph_grouped, ph_raw, tile_of(2))
-        regroup(nc.scalar.copy, ph_grouped, ph_raw, tile_of(3))
-        quantise(nc, ph_codes, ph_scales, ph_grouped, first_half)
-        quantise(nc, ph_codes, ph_scales, ph_grouped, second_half)
+        ph_codes, ph_scales = quantise_weight(nc, keep, ph_raw, "ph")
 
         x_words = x_sb[:].bitcast(F32).rearrange("p a (q u) -> p a u q", u=2)
         x_grouped = keep.tile([P, TOKENS, PACK], BF16, align_bytes=64)
@@ -119,6 +125,10 @@ def tile_quantuminspiredneuralcore_pa_s_kernel(tc, x, amp_w, amp_b, ph_w, ph_b, 
             nc.scalar.copy(
                 out=x_grouped_words[:, tile_of(a), :], in_=x_t[:].rearrange("q u c -> q c u")
             )
+        x_codes = keep.tile([P, TOKENS], U32, align_bytes=64)
+        x_scales = keep.tile([P, TOKENS], U8, align_bytes=64)
+        quantise(nc, x_codes, x_scales, x_grouped, slice(0, HALF))
+        quantise(nc, x_codes, x_scales, x_grouped, slice(HALF, TOKENS))
 
         bias_t = banks.tile([P, P], BF16, tag="bank", name="bias_t")
         nc.tensor.transpose(bias_t[:], bias_rows[:], ident_bf16[:])
@@ -127,11 +137,6 @@ def tile_quantuminspiredneuralcore_pa_s_kernel(tc, x, amp_w, amp_b, ph_w, ph_b, 
         ph_bias = keep.tile([P, FEATURE_TILES], F32)
         nc.scalar.copy(out=ph_bias[:], in_=bias_t[:, FEATURE_TILES : 2 * FEATURE_TILES])
 
-        x_codes = keep.tile([P, TOKENS], U32, align_bytes=64)
-        x_scales = keep.tile([P, TOKENS], U8, align_bytes=64)
-        quantise(nc, x_codes, x_scales, x_grouped, slice(0, HALF))
-        quantise(nc, x_codes, x_scales, x_grouped, slice(HALF, TOKENS))
-
         tanh_ph = keep.tile([P, FEATURE_TILES, TOKENS], F32)
         for f in range(FEATURE_TILES):
             product = multiply(nc, banks, ph_codes, ph_scales, x_codes, x_scales, f, "ph_product")
@@ -139,13 +144,7 @@ def tile_quantuminspiredneuralcore_pa_s_kernel(tc, x, amp_w, amp_b, ph_w, ph_b, 
                 out=tanh_ph[:, f, :], in_=product[:], func=ACT.Tanh, bias=ph_bias[:, f : f + 1]
             )
 
-        amp_grouped = keep.tile([P, FEATURES, PACK], BF16, align_bytes=64)
-        amp_codes = keep.tile([P, FEATURES], U32, align_bytes=64)
-        amp_scales = keep.tile([P, FEATURES], U8, align_bytes=64)
-        regroup(nc.vector.tensor_copy, amp_grouped, amp_raw, first_half)
-        regroup(nc.vector.tensor_copy, amp_grouped, amp_raw, second_half)
-        quantise(nc, amp_codes, amp_scales, amp_grouped, first_half)
-        quantise(nc, amp_codes, amp_scales, amp_grouped, second_half)
+        amp_codes, amp_scales = quantise_weight(nc, keep, amp_raw, "amp")
         tanh_amp = keep.tile([P, FEATURE_TILES, TOKENS], F32)
         for f in range(FEATURE_TILES):
             product = multiply(nc, banks, amp_codes, amp_scales, x_codes, x_scales, f, "amp_product")
@@ -159,55 +158,48 @@ def tile_quantuminspiredneuralcore_pa_s_kernel(tc, x, amp_w, amp_b, ph_w, ph_b, 
 
         mirrored = keep.tile([P, FEATURE_TILES, TOKENS], F32)
         folded = keep.tile([P, FEATURE_TILES, TOKENS], F32)
-        for f in range(FEATURE_TILES):
-            nc.vector.tensor_scalar(
-                out=mirrored[:, f, :],
-                in0=tanh_ph[:, f, :],
-                scalar1=-1.0,
-                scalar2=0.75,
-                op0=ALU.mult,
-                op1=ALU.add,
-            )
-            nc.vector.scalar_tensor_tensor(
-                out=folded[:, f, :],
-                in0=tanh_ph[:, f, :],
-                scalar=0.25,
-                in1=mirrored[:, f, :],
-                op0=ALU.add,
-                op1=ALU.min,
-            )
+        gain = keep.tile([P, FEATURE_TILES, TOKENS], F32)
+        folded_t = []
+        gain_t = []
+        for step in range(FEATURE_TILES + 2):
+            if step < FEATURE_TILES:
+                f = step
+                nc.vector.tensor_scalar(
+                    out=mirrored[:, f, :],
+                    in0=tanh_ph[:, f, :],
+                    scalar1=-1.0,
+                    scalar2=0.75,
+                    op0=ALU.mult,
+                    op1=ALU.add,
+                )
+            if 1 <= step <= FEATURE_TILES:
+                f = step - 1
+                nc.vector.scalar_tensor_tensor(
+                    out=folded[:, f, :],
+                    in0=tanh_ph[:, f, :],
+                    scalar=0.25,
+                    in1=mirrored[:, f, :],
+                    op0=ALU.add,
+                    op1=ALU.min,
+                )
+                folded_t.append(to_token_rows(nc, banks, folded[:, f, :], ident_f32, "folded_t"))
+            if step >= 2:
+                f = step - 2
+                nc.vector.tensor_scalar(
+                    out=gain[:, f, :],
+                    in0=tanh_amp[:, f, :],
+                    scalar1=1.0,
+                    scalar2=1.0 / math.sqrt(2.0),
+                    op0=ALU.add,
+                    op1=ALU.mult,
+                )
+                gain_t.append(to_token_rows(nc, banks, gain[:, f, :], ident_f32, "gain_t"))
 
-        sine = keep.tile([P, FEATURE_TILES, TOKENS], F32)
-        value = keep.tile([P, FEATURE_TILES, TOKENS], F32)
-        value_t = []
-        for f in range(FEATURE_TILES):
-            nc.scalar.activation(
-                out=sine[:, f, :], in_=folded[:, f, :], func=ACT.Sin, scale=math.pi
-            )
-            nc.vector.scalar_tensor_tensor(
-                out=value[:, f, :],
-                in0=tanh_amp[:, f, :],
-                scalar=1.0,
-                in1=sine[:, f, :],
-                op0=ALU.add,
-                op1=ALU.mult,
-            )
-            value_t.append(banks.tile([P, TOKEN_TILES, P], F32, tag="bank", name="value_t"))
-            for a in range(TOKEN_TILES):
-                nc.tensor.transpose(value_t[f][:, a, :], value[:, f, tile_of(a)], ident_f32[:])
-
+        sine = keep.tile([P, FEATURE_TILES, TOKEN_TILES, P], F32)
         result = keep.tile([P, TOKEN_TILES, FEATURES], F32)
         for f in range(FEATURE_TILES):
-            if f < FEATURE_TILES // 2:
-                nc.scalar.mul(
-                    out=result[:, :, tile_of(f)], in_=value_t[f][:], mul=1.0 / math.sqrt(2.0)
-                )
-            else:
-                nc.vector.tensor_scalar(
-                    out=result[:, :, tile_of(f)],
-                    in0=value_t[f][:],
-                    scalar1=1.0 / math.sqrt(2.0),
-                    scalar2=None,
-                    op0=ALU.mult,
-                )
+            nc.scalar.activation(out=sine[:, f], in_=folded_t[f][:], func=ACT.Sin, scale=math.pi)
+            nc.vector.tensor_tensor(
+                out=result[:, :, tile_of(f)], in0=sine[:, f], in1=gain_t[f][:], op=ALU.mult
+            )
             nc.sync.dma_start(out=out_rows[:, :, tile_of(f)], in_=result[:, :, tile_of(f)])

@@ -30,7 +30,10 @@ def tile_of(f):
 
 def load_weight(nc, pool, weight, name):
     raw = pool.tile([P, PACK, FEATURES], BF16, name=name)
-    nc.sync.dma_start(out=raw[:], in_=weight.rearrange("(p t) n -> p t n", t=PACK))
+    nc.sync.dma_start(
+        out=raw[:].rearrange("q (u e) n -> q u (e n)", u=2),
+        in_=weight.rearrange("(u q e) n -> q u (e n)", u=2, e=2),
+    )
     return raw
 
 
@@ -115,7 +118,7 @@ def tile_quantuminspiredneuralcore_pa_s_kernel(tc, x, amp_w, amp_b, ph_w, ph_b, 
 
         ph_codes, ph_scales = quantise_weight(nc, keep, ph_raw, "ph")
 
-        x_words = x_sb[:].bitcast(F32).rearrange("p a (q u) -> p a u q", u=2)
+        x_words = x_sb[:].bitcast(F32).rearrange("p a (u q) -> p a u q", u=2)
         x_grouped = keep.tile([P, TOKENS, PACK], BF16, align_bytes=64)
         x_grouped_words = x_grouped[:].bitcast(F32)
         for a in range(TOKEN_TILES):

import math
from contextlib import ExitStack

import concourse.mybir as mybir
from concourse.masks import make_identity

F32 = mybir.dt.float32
BF16 = mybir.dt.bfloat16
U32 = mybir.dt.uint32
U8 = mybir.dt.uint8
FP8X4 = mybir.dt.float8_e4m3fn_x4
ACT = mybir.ActivationFunctionType
ALU = mybir.AluOpType

P = 128
PACK = 4
K = P * PACK
TOKENS = 384
TOKEN_TILES = TOKENS // P
FEATURES = 512
FEATURE_TILES = FEATURES // P
HALF = 256

FLOPS = 2 * TOKENS * K * 2 * FEATURES


def tile_of(f):
    return slice(f * P, (f + 1) * P)


def load_weight(nc, pool, weight, name):
    raw = pool.tile([P, PACK, FEATURES], BF16, name=name)
    nc.sync.dma_start(
        out=raw[:].rearrange("q (u e) n -> q u (e n)", u=2),
        in_=weight.rearrange("(u q e) n -> q u (e n)", u=2, e=2),
    )
    return raw


def quantise(nc, codes, scales, grouped, cols):
    nc.vector.quantize_mx(
        out=codes[:, cols].bitcast(FP8X4),
        scales=scales[:, cols],
        in_=grouped[:, cols, :].rearrange("p c t -> p (c t)"),
    )


def quantise_weight(nc, pool, raw, name):
    grouped = pool.tile([P, FEATURES, PACK], BF16, name=name + "_grouped", align_bytes=64)
    codes = pool.tile([P, FEATURES], U32, name=name + "_codes", align_bytes=64)
    scales = pool.tile([P, FEATURES], U8, name=name + "_scales", align_bytes=64)
    halves = (slice(0, HALF), slice(HALF, FEATURES))
    for cols in halves:
        nc.vector.tensor_copy(
            out=grouped[:, cols, :].rearrange("p (c i) t -> p c t i", i=4),
            in_=raw[:, :, cols].rearrange("p t (c i) -> p c t i", i=4),
        )
    for cols in halves:
        quantise(nc, codes, scales, grouped, cols)
    return codes, scales


def multiply(nc, banks, w_codes, w_scales, x_codes, x_scales, f, name):
    product = banks.tile([P, TOKENS], F32, tag="bank", name=name)
    for tokens in (slice(0, HALF), slice(HALF, TOKENS)):
        nc.tensor.matmul_mx(
            out=product[:, tokens],
            lhsT=w_codes[:, tile_of(f)].bitcast(FP8X4),
            lhsT_scale=w_scales[:, tile_of(f)],
            rhs=x_codes[:, tokens].bitcast(FP8X4),
            rhs_scale=x_scales[:, tokens],
            start=True,
            stop=True,
        )
    return product


def to_token_rows(nc, banks, values, ident, name):
    transposed = banks.tile([P, TOKEN_TILES, P], F32, tag="bank", name=name)
    for a in range(TOKEN_TILES):
        nc.tensor.transpose(transposed[:, a, :], values[:, tile_of(a)], ident[:])
    return transposed


def tile_quantuminspiredneuralcore_pa_s_kernel(tc, x, amp_w, amp_b, ph_w, ph_b, out):
    nc = tc.nc
    x_rows = x.flatten_outer_dims().rearrange("(p a) k -> p a k", a=TOKEN_TILES)
    out_rows = out.flatten_outer_dims().rearrange("(p a) n -> p a n", a=TOKEN_TILES)

    with ExitStack() as stack:
        keep = stack.enter_context(tc.tile_pool(name="keep", bufs=1))
        banks = stack.enter_context(tc.psum_pool(name="banks", bufs=8))
        stack.enter_context(tc.manual_schedule())

        ph_raw = load_weight(nc, keep, ph_w, "ph_raw")
        x_sb = keep.tile([P, TOKEN_TILES, K], BF16)
        for a in range(TOKEN_TILES):
            nc.sync.dma_start(out=x_sb[:, a, :], in_=x_rows[:, a, :])
        amp_raw = load_weight(nc, keep, amp_w, "amp_raw")
        bias_rows = keep.tile([P, P], BF16)
        nc.vector.memset(bias_rows[:], 0.0)
        nc.scalar.dma_start(
            out=bias_rows[0:FEATURE_TILES, :], in_=amp_b.rearrange("(f c) -> f c", c=P)
        )
        nc.scalar.dma_start(
            out=bias_rows[FEATURE_TILES : 2 * FEATURE_TILES, :],
            in_=ph_b.rearrange("(f c) -> f c", c=P),
        )

        ident_f32 = keep.tile([P, P], F32)
        make_identity(nc, ident_f32[:])
        ident_bf16 = keep.tile([P, P], BF16)
        make_identity(nc, ident_bf16[:])
        one = keep.tile([P, 1], F32)
        nc.vector.memset(one[:], 1.0)
        unused = keep.tile([P, 1], F32)
        nc.scalar.activation(out=unused[:], in_=one[:], func=ACT.Silu)

        ph_codes, ph_scales = quantise_weight(nc, keep, ph_raw, "ph")

        x_words = x_sb[:].bitcast(F32).rearrange("p a (u q) -> p a u q", u=2)
        x_grouped = keep.tile([P, TOKENS, PACK], BF16, align_bytes=64)
        x_grouped_words = x_grouped[:].bitcast(F32)
        for a in range(TOKEN_TILES):
            x_t = banks.tile([P, 2, P], F32, tag="bank", name="x_t")
            for u in range(2):
                nc.tensor.transpose(x_t[:, u, :], x_words[:, a, u, :], ident_f32[:])
            nc.scalar.copy(
                out=x_grouped_words[:, tile_of(a), :], in_=x_t[:].rearrange("q u c -> q c u")
            )
        x_codes = keep.tile([P, TOKENS], U32, align_bytes=64)
        x_scales = keep.tile([P, TOKENS], U8, align_bytes=64)
        quantise(nc, x_codes, x_scales, x_grouped, slice(0, HALF))
        quantise(nc, x_codes, x_scales, x_grouped, slice(HALF, TOKENS))

        bias_t = banks.tile([P, P], BF16, tag="bank", name="bias_t")
        nc.tensor.transpose(bias_t[:], bias_rows[:], ident_bf16[:])
        half_amp_bias = keep.tile([P, FEATURE_TILES], F32)
        nc.scalar.mul(out=half_amp_bias[:], in_=bias_t[:, 0:FEATURE_TILES], mul=0.5)
        ph_bias = keep.tile([P, FEATURE_TILES], F32)
        nc.scalar.copy(out=ph_bias[:], in_=bias_t[:, FEATURE_TILES : 2 * FEATURE_TILES])

        tanh_ph = keep.tile([P, FEATURE_TILES, TOKENS], F32)
        for f in range(FEATURE_TILES):
            product = multiply(nc, banks, ph_codes, ph_scales, x_codes, x_scales, f, "ph_product")
            nc.scalar.activation(
                out=tanh_ph[:, f, :], in_=product[:], func=ACT.Tanh, bias=ph_bias[:, f : f + 1]
            )

        amp_codes, amp_scales = quantise_weight(nc, keep, amp_raw, "amp")
        tanh_amp = keep.tile([P, FEATURE_TILES, TOKENS], F32)
        for f in range(FEATURE_TILES):
            product = multiply(nc, banks, amp_codes, amp_scales, x_codes, x_scales, f, "amp_product")
            nc.scalar.activation(
                out=tanh_amp[:, f, :],
                in_=product[:],
                func=ACT.Tanh,
                bias=half_amp_bias[:, f : f + 1],
                scale=0.5,
            )

        mirrored = keep.tile([P, FEATURE_TILES, TOKENS], F32)
        folded = keep.tile([P, FEATURE_TILES, TOKENS], F32)
        gain = keep.tile([P, FEATURE_TILES, TOKENS], F32)
        folded_t = []
        gain_t = []
        for step in range(FEATURE_TILES + 2):
            if step < FEATURE_TILES:
                f = step
                nc.vector.tensor_scalar(
                    out=mirrored[:, f, :],
                    in0=tanh_ph[:, f, :],
                    scalar1=-1.0,
                    scalar2=0.75,
                    op0=ALU.mult,
                    op1=ALU.add,
                )
            if 1 <= step <= FEATURE_TILES:
                f = step - 1
                nc.vector.scalar_tensor_tensor(
                    out=folded[:, f, :],
                    in0=tanh_ph[:, f, :],
                    scalar=0.25,
                    in1=mirrored[:, f, :],
                    op0=ALU.add,
                    op1=ALU.min,
                )
                folded_t.append(to_token_rows(nc, banks, folded[:, f, :], ident_f32, "folded_t"))
            if step >= 2:
                f = step - 2
                nc.vector.tensor_scalar(
                    out=gain[:, f, :],
                    in0=tanh_amp[:, f, :],
                    scalar1=1.0,
                    scalar2=1.0 / math.sqrt(2.0),
                    op0=ALU.add,
                    op1=ALU.mult,
                )
                gain_t.append(to_token_rows(nc, banks, gain[:, f, :], ident_f32, "gain_t"))

        sine = keep.tile([P, FEATURE_TILES, TOKEN_TILES, P], F32)
        result = keep.tile([P, TOKEN_TILES, FEATURES], F32)
        for f in range(FEATURE_TILES):
            nc.scalar.activation(out=sine[:, f], in_=folded_t[f][:], func=ACT.Sin, scale=math.pi)
            nc.vector.tensor_tensor(
                out=result[:, :, tile_of(f)], in0=sine[:, f], in1=gain_t[f][:], op=ALU.mult
            )
            nc.sync.dma_start(out=out_rows[:, :, tile_of(f)], in_=result[:, :, tile_of(f)])
